import numpy as np
import ml_dtypes


def mxq(x, axis, fmt="e4m3"):
    dtype, down = {"e4m3": (ml_dtypes.float8_e4m3fn, 7), "e5m2": (ml_dtypes.float8_e5m2, 14)}[fmt]
    v = np.moveaxis(np.asarray(x, np.float32).astype(ml_dtypes.bfloat16).astype(np.float64), axis, -1)
    blocks = v.reshape(v.shape[:-1] + (-1, 32))
    amax = np.abs(blocks).max(-1, keepdims=True)
    byte = np.maximum(np.where(amax > 0, np.frexp(amax)[1] - 1 + 127, 0) - down, 1)
    scale = np.exp2(byte - 127.0)
    codes = (blocks / scale).astype(np.float32).astype(dtype).astype(np.float64)
    return np.moveaxis((codes * scale).reshape(v.shape), -1, axis)


WIDE = False


def mx_kscale(k):
    if not WIDE:
        return np.ones(k)
    levels = np.array([10, -10, 5, -5, 0])
    a = np.random.permutation(np.resize(levels, k // 512 * 4)).reshape(k // 512, 4)
    idx = np.arange(k)
    return np.exp2(a[idx // 512, idx % 128 // 32])


BF16 = ml_dtypes.bfloat16


def bf(x):
    return np.asarray(x, np.float32).astype(BF16)


def f64(x):
    return np.asarray(x).astype(np.float64)


E2M1 = np.array([0.0, 0.5, 1.0, 1.5, 2.0, 3.0, 4.0, 6.0, -0.0, -0.5, -1.0, -1.5, -2.0, -3.0, -4.0, -6.0])


def pack_weight(w, fmt):
    k, n = w.shape
    w = f64(bf(w)).reshape(k // 32, 32, n)
    amax = np.abs(w).max(1)
    if fmt == "e4m3":
        byte = np.frexp(amax)[1] - 1 + 127 - 7
    else:
        mant, ex = np.frexp(amax / 6.0)
        byte = np.where(mant > 0.5, ex, ex - 1) + 127
    byte = np.clip(np.where(amax > 0, byte, 1), 1, 254)
    scaled = (w * np.exp2(127.0 - byte)[:, None, :]).reshape(k, n).astype(np.float32)
    by_word = np.ascontiguousarray(scaled.reshape(k // 512, 128, 4, n).transpose(0, 1, 3, 2))
    if fmt == "e4m3":
        words = by_word.astype(ml_dtypes.float8_e4m3fn).view(np.uint8)
    else:
        c = by_word.astype(ml_dtypes.float4_e2m1fn).view(np.uint8) & 0xF
        words = c[..., 0::2] | (c[..., 1::2] << 4)
    return np.ascontiguousarray(words), np.ascontiguousarray(byte.astype(np.uint8).reshape(k // 512, 16, n))


def unpack_weight(words, scales, fmt):
    g, p, n, _ = words.shape
    if fmt == "e4m3":
        vals = np.ascontiguousarray(words).view(ml_dtypes.float8_e4m3fn).astype(np.float64)
    else:
        nib = np.empty((g, p, n, 4), np.uint8)
        nib[..., 0::2] = words & 0xF
        nib[..., 1::2] = words >> 4
        vals = E2M1[nib]
    vals = vals * np.repeat(np.exp2(scales.astype(np.float64) - 127.0), 8, axis=1)[..., None]
    return vals.transpose(0, 1, 3, 2).reshape(g * 512, n)

def pack4(w):
    words, scales = pack_weight(w, "e2m1")
    return words.reshape(words.shape[0], 128, -1), scales


def unpack4(words, scales):
    return unpack_weight(words.reshape(words.shape[0], 128, -1, 2), scales, "e2m1")


B, IN, OUT, POOL_K = 512, 2048, 4096, 4
SCALE = 2.0


def _gelu_tanh(p):
    return 0.5 * p * (1.0 + np.tanh(0.7978845608 * (p + 0.044715 * p * p * p)))


def setup_inputs():
    s = mx_kscale(IN)
    x = bf(np.random.standard_normal((B, IN)) * s)
    weight = np.random.standard_normal((OUT, IN)) * (1.0 / np.sqrt(IN)) / s[None, :]
    words, scales = pack4(np.ascontiguousarray(weight.T))
    bias = bf(np.random.standard_normal(OUT) * 0.5)
    return {"x": x,
            "weight_words": words,
            "weight_scales": scales,
            "bias": bias}


def reference(x, weight_words, weight_scales, bias):
    w = unpack4(weight_words, weight_scales)
    rows = x.shape[0]
    width = w.shape[1]
    y = (mxq(f64(x), 1, "e4m3") @ w) + f64(bias)
    pooled = y.reshape(rows, width // POOL_K, POOL_K).mean(axis=-1)
    scaled = _gelu_tanh(pooled) * SCALE
    return np.max(scaled, axis=1)

@@ -1,0 +1,196 @@
+from contextlib import ExitStack
+
+import concourse.mybir as mybir
+from concourse.masks import make_identity
+
+FLOPS = 2 * 512 * 2048 * 4096
+
+F32 = mybir.dt.float32
+BF16 = mybir.dt.bfloat16
+I32 = mybir.dt.int32
+U8 = mybir.dt.uint8
+U32 = mybir.dt.uint32
+FP8X4 = mybir.dt.float8_e4m3fn_x4
+FP4X4 = mybir.dt.float4_e2m1fn_x4
+ADD = mybir.AluOpType.add
+MAX = mybir.AluOpType.max
+X_AXIS = mybir.AxisListType.X
+GELU = mybir.ActivationFunctionType.Gelu_apprx_tanh
+
+P = 128
+ROWS = 512
+IN = 2048
+OUT = 4096
+POOL = 4
+M_TILES = ROWS // P
+K_PASS = 4 * P
+G = IN // K_PASS
+N_CHUNK = 512
+CHUNKS = OUT // N_CHUNK
+POOLED = N_CHUNK // POOL
+COLUMN_GROUPS = ((0, 1), (1, 1), (2, 2), (4, 2), (6, 2))
+
+
+def tile_modelnew_kernel(tc, x, weight_words, weight_scales, bias, out):
+    nc = tc.nc
+    with ExitStack() as ctx:
+        keep = ctx.enter_context(tc.tile_pool(name="keep", bufs=1))
+        psum = ctx.enter_context(tc.psum_pool(name="psum", bufs=8))
+        ctx.enter_context(tc.manual_schedule())
+
+        warm = keep.tile([P, 1], F32, name="warm")
+        nc.vector.memset(warm[:], 0.0)
+        bias_rows = keep.tile([P, P], BF16, name="bias_rows")
+        nc.scalar.dma_start(
+            out=bias_rows[:],
+            in_=bias.rearrange("(s i) -> s i", i=P).unsqueeze(0).to_broadcast([4, 32, P]),
+        )
+        nc.scalar.activation(out=warm[:], in_=warm[:], func=GELU)
+        ident = keep.tile([P, P], F32, name="ident")
+        make_identity(nc, ident[:])
+
+        x_rows = x.rearrange("(m p) k -> m p k", p=P)
+        x_sb = []
+        for m in range(M_TILES):
+            x_sb.append(keep.tile([P, IN], BF16, name="x_sb%d" % m))
+            nc.sync.dma_start(out=x_sb[m][:], in_=x_rows[m])
+
+        w_tiles = []
+        planes = []
+        for first, count in COLUMN_GROUPS:
+            w_tiles.append(keep.tile([P, G, count * 2 * N_CHUNK], U8, name="w%d" % first, align_bytes=64))
+            planes.append(keep.tile([P, G, count * N_CHUNK], U8, name="plane%d" % first, align_bytes=64))
+            nc.vector.memset(planes[-1][:].bitcast(I32), 0)
+        z = keep.tile([P, P], F32, name="z", align_bytes=64)
+        nc.vector.memset(z[:], 0.0)
+
+        w_i32 = weight_words.bitcast(I32)
+        s_i32 = weight_scales.bitcast(I32)
+        where = {}
+        for i, (first, count) in enumerate(COLUMN_GROUPS):
+            for k in range(count):
+                where[first + k] = (w_tiles[i], planes[i], k)
+            s_lo = first * N_CHUNK // 4
+            s_hi = (first + count) * N_CHUNK // 4
+            for r in range(4):
+                nc.sync.dma_start(
+                    out=planes[i][:].bitcast(I32)[r:P:32],
+                    in_=s_i32[:, r:16:4, s_lo:s_hi].rearrange("g q c -> q g c"),
+                )
+            w_lo = first * 2 * N_CHUNK // 4
+            w_hi = (first + count) * 2 * N_CHUNK // 4
+            if i == 0:
+                for g in range(G):
+                    nc.sync.dma_start(out=w_tiles[i][:, g, :].bitcast(I32), in_=w_i32[g, :, w_lo:w_hi])
+            else:
+                nc.sync.dma_start(
+                    out=w_tiles[i][:].bitcast(I32),
+                    in_=w_i32[:, :, w_lo:w_hi].rearrange("g p b -> p g b"),
+                )
+
+        bias_sum = keep.tile([P, 32], F32, name="bias_sum")
+        nc.vector.tensor_reduce(
+            out=bias_sum[:], in_=bias_rows[:].rearrange("p (b c) -> p b c", c=POOL), axis=X_AXIS, op=ADD
+        )
+        bias_rep = keep.tile([P, 32, 32], F32, name="bias_rep", align_bytes=64)
+        nc.vector.tensor_copy(out=bias_rep[:], in_=bias_sum[:].unsqueeze(2).to_broadcast([P, 32, 32]))
+        bias_t = keep.tile([P, 1024], F32, name="bias_t", align_bytes=64)
+        nc.vector.transpose(out=bias_t[:], in_=bias_rep[:].rearrange("p b r -> p (b r)"))
+
+        codes = keep.tile([P, M_TILES, G * P], U32, name="codes", align_bytes=64)
+        x_scales = keep.tile([P, M_TILES, G * P], U8, name="x_scales", align_bytes=64)
+        for m in range(M_TILES):
+            words = x_sb[m][:].bitcast(F32)
+            grouped = keep.tile([P, G, P, 4], BF16, name="grouped%d" % m, align_bytes=64)
+            for h in range(2):
+                tp = psum.tile([P, 4, P], F32, name="tp", tag="bank")
+                for g2 in range(2):
+                    g = 2 * h + g2
+                    for u in range(2):
+                        nc.tensor.transpose(
+                            out=tp[:, 2 * g2 + u, :],
+                            in_=words[:, 256 * g + u : 256 * (g + 1) : 2],
+                            identity=ident[:],
+                        )
+                nc.scalar.copy(
+                    out=grouped[:].bitcast(F32)[:, 2 * h : 2 * h + 2],
+                    in_=tp[:].rearrange("p (g u) r -> p g r u", u=2),
+                )
+            nc.vector.quantize_mx(
+                out=codes[:, m, :].bitcast(FP8X4),
+                scales=x_scales[:, m, :],
+                in_=grouped[:].rearrange("p g r t -> p (g r t)"),
+            )
+
+        sums = keep.tile([P, M_TILES, OUT // POOL], F32, name="sums")
+        biased = keep.tile([P, M_TILES, OUT // POOL], F32, name="biased")
+        acted = keep.tile([P, M_TILES, OUT // POOL], F32, name="acted")
+        best = keep.tile([P, M_TILES, CHUNKS], F32, name="best")
+
+        def mx_group(n, m):
+            w_tile, plane, k = where[n]
+            acc = psum.tile([P, N_CHUNK], F32, name="acc", tag="bank")
+            for g in range(G):
+                nc.tensor.matmul_mx(
+                    out=acc[:],
+                    lhsT=codes[:, m, g * P : (g + 1) * P].bitcast(FP8X4),
+                    lhsT_scale=x_scales[:, m, g * P : (g + 1) * P],
+                    rhs=w_tile[:, g, k * 2 * N_CHUNK : (k + 1) * 2 * N_CHUNK].bitcast(FP4X4),
+                    rhs_scale=plane[:, g, k * N_CHUNK : (k + 1) * N_CHUNK],
+                    start=(g == 0),
+                    stop=(g == G - 1),
+                )
+            nc.vector.tensor_reduce(
+                out=sums[:, m, n * POOLED : (n + 1) * POOLED],
+                in_=acc[:].rearrange("p (j c) -> p j c", c=POOL),
+                axis=X_AXIS,
+                op=ADD,
+            )
+
+        def cut(t, n, m0, count):
+            return t[:, m0 : m0 + count, n * POOLED : (n + 1) * POOLED]
+
+        def add_bias_and_gelu(engine, n, m0, count):
+            engine.tensor_tensor(
+                out=cut(biased, n, m0, count).rearrange("p m (s b) -> p m s b", b=32),
+                in0=cut(sums, n, m0, count).rearrange("p m (s b) -> p m s b", b=32),
+                in1=bias_t[:]
+                .rearrange("p (b s) -> p s b", s=32)[:, 4 * n : 4 * n + 4, :]
+                .unsqueeze(1)
+                .to_broadcast([P, count, 4, 32]),
+                op=ADD,
+            )
+            nc.scalar.activation(
+                out=cut(acted, n, m0, count), in_=cut(biased, n, m0, count), func=GELU, scale=1.0 / POOL
+            )
+
+        def row_max(n, m0, count):
+            nc.vector.tensor_reduce(
+                out=best[:, m0 : m0 + count, n], in_=cut(acted, n, m0, count), axis=X_AXIS, op=MAX
+            )
+
+        units = []
+        for n in range(CHUNKS):
+            for m0 in (0, 2):
+                units.append((nc.gpsimd, n, m0, 2))
+        units = units[:-1] + [(nc.vector, CHUNKS - 1, 2, 1), (nc.vector, CHUNKS - 1, 3, 1)]
+
+        waiting = None
+        for engine, n, m0, count in units:
+            for m in range(m0, m0 + count):
+                mx_group(n, m)
+            add_bias_and_gelu(engine, n, m0, count)
+            if waiting is not None:
+                row_max(*waiting)
+            waiting = (n, m0, count)
+        row_max(*waiting)
+
+        corner = z[:, 0:P:32]
+        nc.vector.tensor_reduce(out=corner, in_=best[:], axis=X_AXIS, op=MAX)
+        nc.vector.tensor_scalar_mul(out=corner, in0=corner, scalar1=2.0)
+        z_t = keep.tile([P, P], F32, name="z_t", align_bytes=64)
+        nc.vector.transpose(out=z_t[:], in_=z[:])
+        nc.sync.dma_start(
+            out=out.rearrange("(m a r) -> a m r", a=4, r=32),
+            in_=z_t[0:P:32, :].rearrange("a (m r) -> a m r", r=32),
+        )

@@ -28,7 +28,8 @@ G = IN // K_PASS
 N_CHUNK = 512
 CHUNKS = OUT // N_CHUNK
 POOLED = N_CHUNK // POOL
-COLUMN_GROUPS = ((0, 1), (1, 1), (2, 2), (4, 2), (6, 2))
+WEIGHT_LOADS = ((0, 1), (1, 1), (2, 2), (4, 2), (6, 2))
+SCALE_LOADS = ((0, 1), (1, 3), (4, 4))
 
 
 def tile_modelnew_kernel(tc, x, weight_words, weight_scales, bias, out):
@@ -55,10 +56,8 @@ def tile_modelnew_kernel(tc, x, weight_words, weight_scales, bias, out):
             x_sb.append(keep.tile([P, IN], BF16, name="x_sb%d" % m))
             nc.sync.dma_start(out=x_sb[m][:], in_=x_rows[m])
 
-        w_tiles = []
         planes = []
-        for first, count in COLUMN_GROUPS:
-            w_tiles.append(keep.tile([P, G, count * 2 * N_CHUNK], U8, name="w%d" % first, align_bytes=64))
+        for first, count in SCALE_LOADS:
             planes.append(keep.tile([P, G, count * N_CHUNK], U8, name="plane%d" % first, align_bytes=64))
             nc.vector.memset(planes[-1][:].bitcast(I32), 0)
         z = keep.tile([P, P], F32, name="z", align_bytes=64)
@@ -66,27 +65,43 @@ def tile_modelnew_kernel(tc, x, weight_words, weight_scales, bias, out):
 
         w_i32 = weight_words.bitcast(I32)
         s_i32 = weight_scales.bitcast(I32)
-        where = {}
-        for i, (first, count) in enumerate(COLUMN_GROUPS):
+        w_of = {}
+        plane_of = {}
+
+        def load_scales(i):
+            first, count = SCALE_LOADS[i]
             for k in range(count):
-                where[first + k] = (w_tiles[i], planes[i], k)
-            s_lo = first * N_CHUNK // 4
-            s_hi = (first + count) * N_CHUNK // 4
+                plane_of[first + k] = (planes[i], k)
+            lo = first * N_CHUNK // 4
+            hi = (first + count) * N_CHUNK // 4
             for r in range(4):
                 nc.sync.dma_start(
                     out=planes[i][:].bitcast(I32)[r:P:32],
-                    in_=s_i32[:, r:16:4, s_lo:s_hi].rearrange("g q c -> q g c"),
+                    in_=s_i32[:, r:16:4, lo:hi].rearrange("g q c -> q g c"),
                 )
-            w_lo = first * 2 * N_CHUNK // 4
-            w_hi = (first + count) * 2 * N_CHUNK // 4
-            if i == 0:
-                for g in range(G):
-                    nc.sync.dma_start(out=w_tiles[i][:, g, :].bitcast(I32), in_=w_i32[g, :, w_lo:w_hi])
-            else:
+
+        def load_words(i, pieces):
+            first, count = WEIGHT_LOADS[i]
+            w_tile = keep.tile([P, G, count * 2 * N_CHUNK], U8, name="w%d" % first, align_bytes=64)
+            for k in range(count):
+                w_of[first + k] = (w_tile, k)
+            lo = first * 2 * N_CHUNK // 4
+            hi = (first + count) * 2 * N_CHUNK // 4
+            step = G // pieces
+            for g in range(0, G, step):
                 nc.sync.dma_start(
-                    out=w_tiles[i][:].bitcast(I32),
-                    in_=w_i32[:, :, w_lo:w_hi].rearrange("g p b -> p g b"),
+                    out=w_tile[:, g : g + step, :].bitcast(I32),
+                    in_=w_i32[g : g + step, :, lo:hi].rearrange("g p b -> p g b"),
                 )
+
+        load_scales(0)
+        load_words(0, 2)
+        load_scales(1)
+        load_words(1, 1)
+        load_words(2, 1)
+        load_scales(2)
+        load_words(3, 1)
+        load_words(4, 1)
 
         bias_sum = keep.tile([P, 32], F32, name="bias_sum")
         nc.vector.tensor_reduce(
@@ -128,7 +143,8 @@ def tile_modelnew_kernel(tc, x, weight_words, weight_scales, bias, out):
         best = keep.tile([P, M_TILES, CHUNKS], F32, name="best")
 
         def mx_group(n, m):
-            w_tile, plane, k = where[n]
+            w_tile, k = w_of[n]
+            plane, kp = plane_of[n]
             acc = psum.tile([P, N_CHUNK], F32, name="acc", tag="bank")
             for g in range(G):
                 nc.tensor.matmul_mx(
@@ -136,7 +152,7 @@ def tile_modelnew_kernel(tc, x, weight_words, weight_scales, bias, out):
                     lhsT=codes[:, m, g * P : (g + 1) * P].bitcast(FP8X4),
                     lhsT_scale=x_scales[:, m, g * P : (g + 1) * P],
                     rhs=w_tile[:, g, k * 2 * N_CHUNK : (k + 1) * 2 * N_CHUNK].bitcast(FP4X4),
-                    rhs_scale=plane[:, g, k * N_CHUNK : (k + 1) * N_CHUNK],
+                    rhs_scale=plane[:, g, kp * N_CHUNK : (kp + 1) * N_CHUNK],
                     start=(g == 0),
                     stop=(g == G - 1),
                 )

@@ -28,8 +28,8 @@ G = IN // K_PASS
 N_CHUNK = 512
 CHUNKS = OUT // N_CHUNK
 POOLED = N_CHUNK // POOL
-WEIGHT_LOADS = ((0, 1), (1, 1), (2, 2), (4, 2), (6, 2))
-SCALE_LOADS = ((0, 1), (1, 3), (4, 4))
+LAG = 2
+COLUMN_GROUPS = ((0, 1), (1, 1), (2, 2), (4, 2), (6, 2))
 
 
 def tile_modelnew_kernel(tc, x, weight_words, weight_scales, bias, out):
@@ -56,8 +56,10 @@ def tile_modelnew_kernel(tc, x, weight_words, weight_scales, bias, out):
             x_sb.append(keep.tile([P, IN], BF16, name="x_sb%d" % m))
             nc.sync.dma_start(out=x_sb[m][:], in_=x_rows[m])
 
+        w_tiles = []
         planes = []
-        for first, count in SCALE_LOADS:
+        for first, count in COLUMN_GROUPS:
+            w_tiles.append(keep.tile([P, G, count * 2 * N_CHUNK], U8, name="w%d" % first, align_bytes=64))
             planes.append(keep.tile([P, G, count * N_CHUNK], U8, name="plane%d" % first, align_bytes=64))
             nc.vector.memset(planes[-1][:].bitcast(I32), 0)
         z = keep.tile([P, P], F32, name="z", align_bytes=64)
@@ -65,43 +67,27 @@ def tile_modelnew_kernel(tc, x, weight_words, weight_scales, bias, out):
 
         w_i32 = weight_words.bitcast(I32)
         s_i32 = weight_scales.bitcast(I32)
-        w_of = {}
-        plane_of = {}
-
-        def load_scales(i):
-            first, count = SCALE_LOADS[i]
+        where = {}
+        for i, (first, count) in enumerate(COLUMN_GROUPS):
             for k in range(count):
-                plane_of[first + k] = (planes[i], k)
-            lo = first * N_CHUNK // 4
-            hi = (first + count) * N_CHUNK // 4
+                where[first + k] = (w_tiles[i], planes[i], k)
+            s_lo = first * N_CHUNK // 4
+            s_hi = (first + count) * N_CHUNK // 4
             for r in range(4):
                 nc.sync.dma_start(
                     out=planes[i][:].bitcast(I32)[r:P:32],
-                    in_=s_i32[:, r:16:4, lo:hi].rearrange("g q c -> q g c"),
+                    in_=s_i32[:, r:16:4, s_lo:s_hi].rearrange("g q c -> q g c"),
                 )
-
-        def load_words(i, pieces):
-            first, count = WEIGHT_LOADS[i]
-            w_tile = keep.tile([P, G, count * 2 * N_CHUNK], U8, name="w%d" % first, align_bytes=64)
-            for k in range(count):
-                w_of[first + k] = (w_tile, k)
-            lo = first * 2 * N_CHUNK // 4
-            hi = (first + count) * 2 * N_CHUNK // 4
-            step = G // pieces
-            for g in range(0, G, step):
+            w_lo = first * 2 * N_CHUNK // 4
+            w_hi = (first + count) * 2 * N_CHUNK // 4
+            if i == 0:
+                for g in range(G):
+                    nc.sync.dma_start(out=w_tiles[i][:, g, :].bitcast(I32), in_=w_i32[g, :, w_lo:w_hi])
+            else:
                 nc.sync.dma_start(
-                    out=w_tile[:, g : g + step, :].bitcast(I32),
-                    in_=w_i32[g : g + step, :, lo:hi].rearrange("g p b -> p g b"),
+                    out=w_tiles[i][:].bitcast(I32),
+                    in_=w_i32[:, :, w_lo:w_hi].rearrange("g p b -> p g b"),
                 )
-
-        load_scales(0)
-        load_words(0, 2)
-        load_scales(1)
-        load_words(1, 1)
-        load_words(2, 1)
-        load_scales(2)
-        load_words(3, 1)
-        load_words(4, 1)
 
         bias_sum = keep.tile([P, 32], F32, name="bias_sum")
         nc.vector.tensor_reduce(
@@ -127,7 +113,8 @@ def tile_modelnew_kernel(tc, x, weight_words, weight_scales, bias, out):
                             in_=words[:, 256 * g + u : 256 * (g + 1) : 2],
                             identity=ident[:],
                         )
-                nc.scalar.copy(
+                copy_out = nc.vector.tensor_copy if h == 0 else nc.scalar.copy
+                copy_out(
                     out=grouped[:].bitcast(F32)[:, 2 * h : 2 * h + 2],
                     in_=tp[:].rearrange("p (g u) r -> p g r u", u=2),
                 )
@@ -143,8 +130,7 @@ def tile_modelnew_kernel(tc, x, weight_words, weight_scales, bias, out):
         best = keep.tile([P, M_TILES, CHUNKS], F32, name="best")
 
         def mx_group(n, m):
-            w_tile, k = w_of[n]
-            plane, kp = plane_of[n]
+            w_tile, plane, k = where[n]
             acc = psum.tile([P, N_CHUNK], F32, name="acc", tag="bank")
             for g in range(G):
                 nc.tensor.matmul_mx(
@@ -152,7 +138,7 @@ def tile_modelnew_kernel(tc, x, weight_words, weight_scales, bias, out):
                     lhsT=codes[:, m, g * P : (g + 1) * P].bitcast(FP8X4),
                     lhsT_scale=x_scales[:, m, g * P : (g + 1) * P],
                     rhs=w_tile[:, g, k * 2 * N_CHUNK : (k + 1) * 2 * N_CHUNK].bitcast(FP4X4),
-                    rhs_scale=plane[:, g, kp * N_CHUNK : (kp + 1) * N_CHUNK],
+                    rhs_scale=plane[:, g, k * N_CHUNK : (k + 1) * N_CHUNK],
                     start=(g == 0),
                     stop=(g == G - 1),
                 )
@@ -191,15 +177,16 @@ def tile_modelnew_kernel(tc, x, weight_words, weight_scales, bias, out):
                 units.append((nc.gpsimd, n, m0, 2))
         units = units[:-1] + [(nc.vector, CHUNKS - 1, 2, 1), (nc.vector, CHUNKS - 1, 3, 1)]
 
-        waiting = None
+        waiting = []
         for engine, n, m0, count in units:
             for m in range(m0, m0 + count):
                 mx_group(n, m)
             add_bias_and_gelu(engine, n, m0, count)
-            if waiting is not None:
-                row_max(*waiting)
-            waiting = (n, m0, count)
-        row_max(*waiting)
+            waiting.append((n, m0, count))
+            if len(waiting) > LAG:
+                row_max(*waiting.pop(0))
+        for unit in waiting:
+            row_max(*unit)
 
         corner = z[:, 0:P:32]
         nc.vector.tensor_reduce(out=corner, in_=best[:], axis=X_AXIS, op=MAX)

@@ -37,7 +37,6 @@ def tile_modelnew_kernel(tc, x, weight_words, weight_scales, bias, out):
     with ExitStack() as ctx:
         keep = ctx.enter_context(tc.tile_pool(name="keep", bufs=1))
         psum = ctx.enter_context(tc.psum_pool(name="psum", bufs=8))
-        ctx.enter_context(tc.manual_schedule())
 
         warm = keep.tile([P, 1], F32, name="warm")
         nc.vector.memset(warm[:], 0.0)

@@ -28,6 +28,7 @@ G = IN // K_PASS
 N_CHUNK = 512
 CHUNKS = OUT // N_CHUNK
 POOLED = N_CHUNK // POOL
+PAD_WORDS = 48
 LAG = 2
 COLUMN_GROUPS = ((0, 1), (1, 1), (2, 2), (4, 2), (6, 2))
 
@@ -37,6 +38,7 @@ def tile_modelnew_kernel(tc, x, weight_words, weight_scales, bias, out):
     with ExitStack() as ctx:
         keep = ctx.enter_context(tc.tile_pool(name="keep", bufs=1))
         psum = ctx.enter_context(tc.psum_pool(name="psum", bufs=8))
+        ctx.enter_context(tc.manual_schedule())
 
         warm = keep.tile([P, 1], F32, name="warm")
         nc.vector.memset(warm[:], 0.0)
@@ -58,8 +60,8 @@ def tile_modelnew_kernel(tc, x, weight_words, weight_scales, bias, out):
         w_tiles = []
         planes = []
         for first, count in COLUMN_GROUPS:
-            w_tiles.append(keep.tile([P, G, count * 2 * N_CHUNK], U8, name="w%d" % first, align_bytes=64))
-            planes.append(keep.tile([P, G, count * N_CHUNK], U8, name="plane%d" % first, align_bytes=64))
+            w_tiles.append(keep.tile([P, G, count * 2 * N_CHUNK], U8, name="w%d" % first, align_bytes=256))
+            planes.append(keep.tile([P, G, count * N_CHUNK], U8, name="plane%d" % first, align_bytes=256))
             nc.vector.memset(planes[-1][:].bitcast(I32), 0)
         z = keep.tile([P, P], F32, name="z", align_bytes=64)
         nc.vector.memset(z[:], 0.0)
@@ -97,8 +99,16 @@ def tile_modelnew_kernel(tc, x, weight_words, weight_scales, bias, out):
         bias_t = keep.tile([P, 1024], F32, name="bias_t", align_bytes=64)
         nc.vector.transpose(out=bias_t[:], in_=bias_rep[:].rearrange("p b r -> p (b r)"))
 
-        codes = keep.tile([P, M_TILES, G * P], U32, name="codes", align_bytes=64)
-        x_scales = keep.tile([P, M_TILES, G * P], U8, name="x_scales", align_bytes=64)
+        codes = keep.tile([P, PAD_WORDS + M_TILES * G * P], U32, name="codes", align_bytes=256)
+        x_scales = keep.tile([P, M_TILES * G, 2 * P], U8, name="x_scales", align_bytes=256)
+
+        def x_codes(m, g):
+            lo = PAD_WORDS + (m * G + g) * P
+            return codes[:, lo : lo + P].bitcast(FP8X4)
+
+        def x_plane(m, g):
+            return x_scales[:, m * G + g, 0:P]
+
         for m in range(M_TILES):
             words = x_sb[m][:].bitcast(F32)
             grouped = keep.tile([P, G, P, 4], BF16, name="grouped%d" % m, align_bytes=64)
@@ -117,11 +127,10 @@ def tile_modelnew_kernel(tc, x, weight_words, weight_scales, bias, out):
                     out=grouped[:].bitcast(F32)[:, 2 * h : 2 * h + 2],
                     in_=tp[:].rearrange("p (g u) r -> p g r u", u=2),
                 )
-            nc.vector.quantize_mx(
-                out=codes[:, m, :].bitcast(FP8X4),
-                scales=x_scales[:, m, :],
-                in_=grouped[:].rearrange("p g r t -> p (g r t)"),
-            )
+            for g in range(G):
+                nc.vector.quantize_mx(
+                    out=x_codes(m, g), scales=x_plane(m, g), in_=grouped[:, g].rearrange("p r t -> p (r t)")
+                )
 
         sums = keep.tile([P, M_TILES, OUT // POOL], F32, name="sums")
         biased = keep.tile([P, M_TILES, OUT // POOL], F32, name="biased")
@@ -134,8 +143,8 @@ def tile_modelnew_kernel(tc, x, weight_words, weight_scales, bias, out):
             for g in range(G):
                 nc.tensor.matmul_mx(
                     out=acc[:],
-                    lhsT=codes[:, m, g * P : (g + 1) * P].bitcast(FP8X4),
-                    lhsT_scale=x_scales[:, m, g * P : (g + 1) * P],
+                    lhsT=x_codes(m, g),
+                    lhsT_scale=x_plane(m, g),
                     rhs=w_tile[:, g, k * 2 * N_CHUNK : (k + 1) * 2 * N_CHUNK].bitcast(FP4X4),
                     rhs_scale=plane[:, g, k * N_CHUNK : (k + 1) * N_CHUNK],
                     start=(g == 0),

@@ -42,11 +42,6 @@ def tile_modelnew_kernel(tc, x, weight_words, weight_scales, bias, out):
 
         warm = keep.tile([P, 1], F32, name="warm")
         nc.vector.memset(warm[:], 0.0)
-        bias_rows = keep.tile([P, P], BF16, name="bias_rows")
-        nc.scalar.dma_start(
-            out=bias_rows[:],
-            in_=bias.rearrange("(s i) -> s i", i=P).unsqueeze(0).to_broadcast([4, 32, P]),
-        )
         nc.scalar.activation(out=warm[:], in_=warm[:], func=GELU)
         ident = keep.tile([P, P], F32, name="ident")
         make_identity(nc, ident[:])
@@ -66,6 +61,7 @@ def tile_modelnew_kernel(tc, x, weight_words, weight_scales, bias, out):
         z = keep.tile([P, P], F32, name="z", align_bytes=64)
         nc.vector.memset(z[:], 0.0)
 
+        bias_rows = keep.tile([P, P], BF16, name="bias_rows")
         w_i32 = weight_words.bitcast(I32)
         s_i32 = weight_scales.bitcast(I32)
         where = {}
@@ -84,20 +80,15 @@ def tile_modelnew_kernel(tc, x, weight_words, weight_scales, bias, out):
             if i == 0:
                 for g in range(G):
                     nc.sync.dma_start(out=w_tiles[i][:, g, :].bitcast(I32), in_=w_i32[g, :, w_lo:w_hi])
+                nc.sync.dma_start(
+                    out=bias_rows[:],
+                    in_=bias.rearrange("(s i) -> s i", i=P).unsqueeze(0).to_broadcast([4, 32, P]),
+                )
             else:
                 nc.sync.dma_start(
                     out=w_tiles[i][:].bitcast(I32),
                     in_=w_i32[:, :, w_lo:w_hi].rearrange("g p b -> p g b"),
                 )
-
-        bias_sum = keep.tile([P, 32], F32, name="bias_sum")
-        nc.vector.tensor_reduce(
-            out=bias_sum[:], in_=bias_rows[:].rearrange("p (b c) -> p b c", c=POOL), axis=X_AXIS, op=ADD
-        )
-        bias_rep = keep.tile([P, 32, 32], F32, name="bias_rep", align_bytes=64)
-        nc.vector.tensor_copy(out=bias_rep[:], in_=bias_sum[:].unsqueeze(2).to_broadcast([P, 32, 32]))
-        bias_t = keep.tile([P, 1024], F32, name="bias_t", align_bytes=64)
-        nc.vector.transpose(out=bias_t[:], in_=bias_rep[:].rearrange("p b r -> p (b r)"))
 
         codes = keep.tile([P, PAD_WORDS + M_TILES * G * P], U32, name="codes", align_bytes=256)
         x_scales = keep.tile([P, M_TILES * G, 2 * P], U8, name="x_scales", align_bytes=256)
@@ -131,6 +122,15 @@ def tile_modelnew_kernel(tc, x, weight_words, weight_scales, bias, out):
                 nc.vector.quantize_mx(
                     out=x_codes(m, g), scales=x_plane(m, g), in_=grouped[:, g].rearrange("p r t -> p (r t)")
                 )
+
+        bias_sum = keep.tile([P, 32], F32, name="bias_sum")
+        nc.vector.tensor_reduce(
+            out=bias_sum[:], in_=bias_rows[:].rearrange("p (b c) -> p b c", c=POOL), axis=X_AXIS, op=ADD
+        )
+        bias_rep = keep.tile([P, 32, 32], F32, name="bias_rep", align_bytes=64)
+        nc.vector.tensor_copy(out=bias_rep[:], in_=bias_sum[:].unsqueeze(2).to_broadcast([P, 32, 32]))
+        bias_t = keep.tile([P, 1024], F32, name="bias_t", align_bytes=64)
+        nc.vector.transpose(out=bias_t[:], in_=bias_rep[:].rearrange("p b r -> p (b r)"))
 
         sums = keep.tile([P, M_TILES, OUT // POOL], F32, name="sums")
         biased = keep.tile([P, M_TILES, OUT // POOL], F32, name="biased")

@@ -14,6 +14,7 @@ FP8X4 = mybir.dt.float8_e4m3fn_x4
 FP4X4 = mybir.dt.float4_e2m1fn_x4
 ADD = mybir.AluOpType.add
 MAX = mybir.AluOpType.max
+MULT = mybir.AluOpType.mult
 X_AXIS = mybir.AxisListType.X
 GELU = mybir.ActivationFunctionType.Gelu_apprx_tanh
 
@@ -29,8 +30,14 @@ N_CHUNK = 512
 CHUNKS = OUT // N_CHUNK
 POOLED = N_CHUNK // POOL
 PAD_WORDS = 48
+TAPER = 128
+CATCH_UP = 14
 LAG = 2
 COLUMN_GROUPS = ((0, 1), (1, 1), (2, 2), (4, 2), (6, 2))
+
+
+def TAIL_ENGINE(nc):
+    return nc.vector
 
 
 def tile_modelnew_kernel(tc, x, weight_words, weight_scales, bias, out):
@@ -137,68 +144,92 @@ def tile_modelnew_kernel(tc, x, weight_words, weight_scales, bias, out):
         acted = keep.tile([P, M_TILES, OUT // POOL], F32, name="acted")
         best = keep.tile([P, M_TILES, CHUNKS], F32, name="best")
 
-        def mx_group(n, m):
-            w_tile, plane, k = where[n]
-            acc = psum.tile([P, N_CHUNK], F32, name="acc", tag="bank")
+        def mx_group(m, col, width):
+            w_tile, plane, k = where[col // N_CHUNK]
+            lo = k * N_CHUNK + col % N_CHUNK
+            acc = psum.tile([P, width], F32, name="acc", tag="bank")
             for g in range(G):
                 nc.tensor.matmul_mx(
                     out=acc[:],
                     lhsT=x_codes(m, g),
                     lhsT_scale=x_plane(m, g),
-                    rhs=w_tile[:, g, k * 2 * N_CHUNK : (k + 1) * 2 * N_CHUNK].bitcast(FP4X4),
-                    rhs_scale=plane[:, g, k * N_CHUNK : (k + 1) * N_CHUNK],
+                    rhs=w_tile[:, g, 2 * lo : 2 * (lo + width)].bitcast(FP4X4),
+                    rhs_scale=plane[:, g, lo : lo + width],
                     start=(g == 0),
                     stop=(g == G - 1),
                 )
             nc.vector.tensor_reduce(
-                out=sums[:, m, n * POOLED : (n + 1) * POOLED],
+                out=sums[:, m, col // POOL : (col + width) // POOL],
                 in_=acc[:].rearrange("p (j c) -> p j c", c=POOL),
                 axis=X_AXIS,
                 op=ADD,
             )
 
-        def cut(t, n, m0, count):
-            return t[:, m0 : m0 + count, n * POOLED : (n + 1) * POOLED]
-
-        def add_bias_and_gelu(engine, n, m0, count):
+        def add_bias_and_gelu(engine, m0, count, j0, j1):
             engine.tensor_tensor(
-                out=cut(biased, n, m0, count).rearrange("p m (s b) -> p m s b", b=32),
-                in0=cut(sums, n, m0, count).rearrange("p m (s b) -> p m s b", b=32),
+                out=biased[:, m0 : m0 + count, j0:j1].rearrange("p m (s b) -> p m s b", b=32),
+                in0=sums[:, m0 : m0 + count, j0:j1].rearrange("p m (s b) -> p m s b", b=32),
                 in1=bias_t[:]
-                .rearrange("p (b s) -> p s b", s=32)[:, 4 * n : 4 * n + 4, :]
+                .rearrange("p (b s) -> p s b", s=32)[:, j0 // 32 : j1 // 32, :]
                 .unsqueeze(1)
-                .to_broadcast([P, count, 4, 32]),
+                .to_broadcast([P, count, (j1 - j0) // 32, 32]),
                 op=ADD,
             )
             nc.scalar.activation(
-                out=cut(acted, n, m0, count), in_=cut(biased, n, m0, count), func=GELU, scale=1.0 / POOL
+                out=acted[:, m0 : m0 + count, j0:j1],
+                in_=biased[:, m0 : m0 + count, j0:j1],
+                func=GELU,
+                scale=1.0 / POOL,
             )
 
-        def row_max(n, m0, count):
-            nc.vector.tensor_reduce(
-                out=best[:, m0 : m0 + count, n], in_=cut(acted, n, m0, count), axis=X_AXIS, op=MAX
-            )
+        def row_max(target, m0, count, j0, j1):
+            nc.vector.tensor_reduce(out=target, in_=acted[:, m0 : m0 + count, j0:j1], axis=X_AXIS, op=MAX)
 
+        last = keep.tile([P, 1], F32, name="last")
         units = []
         for n in range(CHUNKS):
             for m0 in (0, 2):
-                units.append((nc.gpsimd, n, m0, 2))
-        units = units[:-1] + [(nc.vector, CHUNKS - 1, 2, 1), (nc.vector, CHUNKS - 1, 3, 1)]
+                units.append(
+                    (
+                        nc.gpsimd,
+                        [(m0, n * N_CHUNK, N_CHUNK), (m0 + 1, n * N_CHUNK, N_CHUNK)],
+                        best[:, m0 : m0 + 2, n],
+                        (m0, 2, n * POOLED, (n + 1) * POOLED),
+                    )
+                )
+        end = OUT - N_CHUNK
+        units = units[:-1] + [
+            (nc.gpsimd, [(2, end, N_CHUNK)], best[:, 2:3, CHUNKS - 1], (2, 1, end // POOL, OUT // POOL)),
+            (
+                TAIL_ENGINE(nc),
+                [(3, end + q * TAPER, TAPER) for q in range(3)],
+                best[:, 3:4, CHUNKS - 1],
+                (3, 1, end // POOL, (OUT - TAPER) // POOL),
+            ),
+            (nc.vector, [(3, OUT - TAPER, TAPER)], last[:], (3, 1, (OUT - TAPER) // POOL, OUT // POOL)),
+        ]
 
         waiting = []
-        for engine, n, m0, count in units:
-            for m in range(m0, m0 + count):
-                mx_group(n, m)
-            add_bias_and_gelu(engine, n, m0, count)
-            waiting.append((n, m0, count))
-            if len(waiting) > LAG:
-                row_max(*waiting.pop(0))
-        for unit in waiting:
-            row_max(*unit)
+        for i, (engine, groups, target, span) in enumerate(units):
+            for m, col, width in groups:
+                mx_group(m, col, width)
+            add_bias_and_gelu(engine, *span)
+            waiting.append((target, span))
+            lag = LAG if i < CATCH_UP else (1 if i == CATCH_UP else len(units))
+            while len(waiting) > lag:
+                target, span = waiting.pop(0)
+                row_max(target, *span)
 
         corner = z[:, 0:P:32]
+        for target, span in waiting[:-1]:
+            row_max(target, *span)
         nc.vector.tensor_reduce(out=corner, in_=best[:], axis=X_AXIS, op=MAX)
         nc.vector.tensor_scalar_mul(out=corner, in0=corner, scalar1=2.0)
+        target, span = waiting[-1]
+        row_max(target, *span)
+        nc.vector.tensor_scalar(
+            out=z[:, 96:97], in0=last[:], scalar1=2.0, scalar2=z[:, 96:97], op0=MULT, op1=MAX
+        )
         z_t = keep.tile([P, P], F32, name="z_t", align_bytes=64)
         nc.vector.transpose(out=z_t[:], in_=z[:])
         nc.sync.dma_start(

@@ -31,13 +31,11 @@ CHUNKS = OUT // N_CHUNK
 POOLED = N_CHUNK // POOL
 PAD_WORDS = 48
 TAPER = 128
-CATCH_UP = 14
 LAG = 2
-COLUMN_GROUPS = ((0, 1), (1, 1), (2, 2), (4, 2), (6, 2))
-
-
-def TAIL_ENGINE(nc):
-    return nc.vector
+Q = 32
+PLANE_GROUPS = ((0, 1), (1, 1), (2, 2), (4, 4))
+LATE_AFTER = {5: 2, 7: 3}
+LATE_STEPS = {2: (4, 5, 5, 6), 3: (8, 9, 9, 10)}
 
 
 def tile_modelnew_kernel(tc, x, weight_words, weight_scales, bias, out):
@@ -55,50 +53,67 @@ def tile_modelnew_kernel(tc, x, weight_words, weight_scales, bias, out):
 
         x_rows = x.rearrange("(m p) k -> m p k", p=P)
         x_sb = []
-        for m in range(M_TILES):
+        for m in (0, 1):
             x_sb.append(keep.tile([P, IN], BF16, name="x_sb%d" % m))
             nc.sync.dma_start(out=x_sb[m][:], in_=x_rows[m])
 
         w_tiles = []
-        planes = []
-        for first, count in COLUMN_GROUPS:
-            w_tiles.append(keep.tile([P, G, count * 2 * N_CHUNK], U8, name="w%d" % first, align_bytes=256))
-            planes.append(keep.tile([P, G, count * N_CHUNK], U8, name="plane%d" % first, align_bytes=256))
-            nc.vector.memset(planes[-1][:].bitcast(I32), 0)
+        for c in range(CHUNKS):
+            w_tiles.append(keep.tile([P, G, 2 * N_CHUNK], U8, name="w%d" % c, align_bytes=256))
+        planes = {}
+        plane_tiles = {}
+        for first, count in PLANE_GROUPS:
+            plane_tiles[first] = keep.tile([P, G, count * N_CHUNK], U8, name="plane%d" % first, align_bytes=256)
+            nc.vector.memset(plane_tiles[first][:].bitcast(I32), 0)
+            for k in range(count):
+                planes[first + k] = (plane_tiles[first], k)
         z = keep.tile([P, P], F32, name="z", align_bytes=64)
         nc.vector.memset(z[:], 0.0)
 
         bias_rows = keep.tile([P, P], BF16, name="bias_rows")
         w_i32 = weight_words.bitcast(I32)
         s_i32 = weight_scales.bitcast(I32)
-        where = {}
-        for i, (first, count) in enumerate(COLUMN_GROUPS):
-            for k in range(count):
-                where[first + k] = (w_tiles[i], planes[i], k)
-            s_lo = first * N_CHUNK // 4
-            s_hi = (first + count) * N_CHUNK // 4
-            for r in range(4):
-                nc.sync.dma_start(
-                    out=planes[i][:].bitcast(I32)[r:P:32],
-                    in_=s_i32[:, r:16:4, s_lo:s_hi].rearrange("g q c -> q g c"),
-                )
-            w_lo = first * 2 * N_CHUNK // 4
-            w_hi = (first + count) * 2 * N_CHUNK // 4
-            if i == 0:
-                for g in range(G):
-                    nc.sync.dma_start(out=w_tiles[i][:, g, :].bitcast(I32), in_=w_i32[g, :, w_lo:w_hi])
+        x_blocks = x.rearrange("r k -> (r k)").rearrange(
+            "(m j y a e) -> m a j y e", m=M_TILES, j=Q, y=4 * G, a=P // Q
+        )
+        x_late = {}
+        for c in range(CHUNKS):
+            if c in plane_tiles:
+                s_lo = c * N_CHUNK // 4
+                s_hi = s_lo + plane_tiles[c].shape[2] // 4
+                for r in range(4):
+                    nc.sync.dma_start(
+                        out=plane_tiles[c][:].bitcast(I32)[r:P:32],
+                        in_=s_i32[:, r:16:4, s_lo:s_hi].rearrange("g q c -> q g c"),
+                    )
+            w_lo = c * 2 * N_CHUNK // 4
+            w_hi = (c + 1) * 2 * N_CHUNK // 4
+            if c == 0:
+                for g in range(0, G, 2):
+                    nc.sync.dma_start(
+                        out=w_tiles[c][:, g : g + 2, :].bitcast(I32),
+                        in_=w_i32[g : g + 2, :, w_lo:w_hi].rearrange("g p b -> p g b"),
+                    )
                 nc.sync.dma_start(
                     out=bias_rows[:],
                     in_=bias.rearrange("(s i) -> s i", i=P).unsqueeze(0).to_broadcast([4, 32, P]),
                 )
             else:
                 nc.sync.dma_start(
-                    out=w_tiles[i][:].bitcast(I32),
+                    out=w_tiles[c][:].bitcast(I32),
                     in_=w_i32[:, :, w_lo:w_hi].rearrange("g p b -> p g b"),
                 )
+            if c in LATE_AFTER:
+                m = LATE_AFTER[c]
+                x_late[m] = keep.tile([P, 4 * G, P], BF16, name="x_late%d" % m, align_bytes=64)
+                for a in range(P // Q):
+                    nc.sync.dma_start(out=x_late[m][Q * a : Q * (a + 1)], in_=x_blocks[m, a])
 
         codes = keep.tile([P, PAD_WORDS + M_TILES * G * P], U32, name="codes", align_bytes=256)
         x_scales = keep.tile([P, M_TILES * G, 2 * P], U8, name="x_scales", align_bytes=256)
+        grouped = []
+        for m in range(M_TILES):
+            grouped.append(keep.tile([P, G, P, 4], BF16, name="grouped%d" % m, align_bytes=64))
 
         def x_codes(m, g):
             lo = PAD_WORDS + (m * G + g) * P
@@ -107,9 +122,14 @@ def tile_modelnew_kernel(tc, x, weight_words, weight_scales, bias, out):
         def x_plane(m, g):
             return x_scales[:, m * G + g, 0:P]
 
-        for m in range(M_TILES):
+        def quantise(m):
+            for g in range(G):
+                nc.vector.quantize_mx(
+                    out=x_codes(m, g), scales=x_plane(m, g), in_=grouped[m][:, g].rearrange("p r t -> p (r t)")
+                )
+
+        for m in (0, 1):
             words = x_sb[m][:].bitcast(F32)
-            grouped = keep.tile([P, G, P, 4], BF16, name="grouped%d" % m, align_bytes=64)
             for h in range(2):
                 tp = psum.tile([P, 4, P], F32, name="tp", tag="bank")
                 for g2 in range(2):
@@ -122,13 +142,33 @@ def tile_modelnew_kernel(tc, x, weight_words, weight_scales, bias, out):
                         )
                 copy_out = nc.vector.tensor_copy if h == 0 else nc.scalar.copy
                 copy_out(
-                    out=grouped[:].bitcast(F32)[:, 2 * h : 2 * h + 2],
+                    out=grouped[m][:].bitcast(F32)[:, 2 * h : 2 * h + 2],
                     in_=tp[:].rearrange("p (g u) r -> p g r u", u=2),
                 )
+            quantise(m)
+
+        split = {}
+        turned = {}
+
+        def late_split(m):
+            split[m] = keep.tile([P, 4 * G, 2, Q], F32, name="split%d" % m, align_bytes=64)
+            words = x_late[m][:].rearrange("p y e -> p (y e)").bitcast(F32)
+            nc.scalar.copy(out=split[m][:], in_=words.rearrange("p (y i u) -> p y u i", i=Q, u=2))
+
+        def late_turn(m):
+            turned[m] = keep.tile([P, 4 * G * 2 * Q], F32, name="turned%d" % m, align_bytes=64)
+            nc.vector.transpose(out=turned[m][:], in_=split[m][:].rearrange("p y u i -> p (y u i)"))
+
+        def late_group(m):
+            source = turned[m][:].rearrange("p (b g u j) -> p g j b u", b=4, g=G, u=2)
+            target = grouped[m][:].bitcast(F32)
             for g in range(G):
-                nc.vector.quantize_mx(
-                    out=x_codes(m, g), scales=x_plane(m, g), in_=grouped[:, g].rearrange("p r t -> p (r t)")
-                )
+                nc.scalar.copy(out=target[:, g].rearrange("p (j b) u -> p j b u", b=4), in_=source[:, g])
+
+        late_calls = {}
+        for m in LATE_STEPS:
+            for step, call in zip(LATE_STEPS[m], (late_split, late_turn, late_group, quantise)):
+                late_calls.setdefault(step, []).append((call, m))
 
         bias_sum = keep.tile([P, 32], F32, name="bias_sum")
         nc.vector.tensor_reduce(
@@ -145,16 +185,17 @@ def tile_modelnew_kernel(tc, x, weight_words, weight_scales, bias, out):
         best = keep.tile([P, M_TILES, CHUNKS], F32, name="best")
 
         def mx_group(m, col, width):
-            w_tile, plane, k = where[col // N_CHUNK]
-            lo = k * N_CHUNK + col % N_CHUNK
+            c = col // N_CHUNK
+            lo = col % N_CHUNK
+            plane, k = planes[c]
             acc = psum.tile([P, width], F32, name="acc", tag="bank")
             for g in range(G):
                 nc.tensor.matmul_mx(
                     out=acc[:],
                     lhsT=x_codes(m, g),
                     lhsT_scale=x_plane(m, g),
-                    rhs=w_tile[:, g, 2 * lo : 2 * (lo + width)].bitcast(FP4X4),
-                    rhs_scale=plane[:, g, lo : lo + width],
+                    rhs=w_tiles[c][:, g, 2 * lo : 2 * (lo + width)].bitcast(FP4X4),
+                    rhs_scale=plane[:, g, k * N_CHUNK + lo : k * N_CHUNK + lo + width],
                     start=(g == 0),
                     stop=(g == G - 1),
                 )
@@ -182,51 +223,55 @@ def tile_modelnew_kernel(tc, x, weight_words, weight_scales, bias, out):
                 scale=1.0 / POOL,
             )
 
-        def row_max(target, m0, count, j0, j1):
-            nc.vector.tensor_reduce(out=target, in_=acted[:, m0 : m0 + count, j0:j1], axis=X_AXIS, op=MAX)
+        def row_max(m0, count, j0, j1):
+            nc.vector.tensor_reduce(
+                out=best[:, m0 : m0 + count, j0 // POOLED : j1 // POOLED],
+                in_=acted[:, m0 : m0 + count, j0:j1].rearrange("p m (n j) -> p m n j", j=POOLED),
+                axis=X_AXIS,
+                op=MAX,
+            )
 
-        last = keep.tile([P, 1], F32, name="last")
         units = []
         for n in range(CHUNKS):
-            for m0 in (0, 2):
-                units.append(
-                    (
-                        nc.gpsimd,
-                        [(m0, n * N_CHUNK, N_CHUNK), (m0 + 1, n * N_CHUNK, N_CHUNK)],
-                        best[:, m0 : m0 + 2, n],
-                        (m0, 2, n * POOLED, (n + 1) * POOLED),
-                    )
-                )
-        end = OUT - N_CHUNK
-        units = units[:-1] + [
-            (nc.gpsimd, [(2, end, N_CHUNK)], best[:, 2:3, CHUNKS - 1], (2, 1, end // POOL, OUT // POOL)),
-            (
-                TAIL_ENGINE(nc),
-                [(3, end + q * TAPER, TAPER) for q in range(3)],
-                best[:, 3:4, CHUNKS - 1],
-                (3, 1, end // POOL, (OUT - TAPER) // POOL),
-            ),
-            (nc.vector, [(3, OUT - TAPER, TAPER)], last[:], (3, 1, (OUT - TAPER) // POOL, OUT // POOL)),
-        ]
+            units.append((((0, n), (1, n)), (0, 2, n * POOLED, (n + 1) * POOLED)))
+        for m in (2, 3):
+            for n in range(0, CHUNKS, 2):
+                units.append((((m, n), (m, n + 1)), (m, 1, n * POOLED, (n + 2) * POOLED)))
+        units = units[:-1]
 
         waiting = []
-        for i, (engine, groups, target, span) in enumerate(units):
-            for m, col, width in groups:
-                mx_group(m, col, width)
-            add_bias_and_gelu(engine, *span)
-            waiting.append((target, span))
-            lag = LAG if i < CATCH_UP else (1 if i == CATCH_UP else len(units))
-            while len(waiting) > lag:
-                target, span = waiting.pop(0)
-                row_max(target, *span)
+        for i, (pair, span) in enumerate(units):
+            for m, n in pair:
+                mx_group(m, n * N_CHUNK, N_CHUNK)
+            add_bias_and_gelu(nc.gpsimd, *span)
+            waiting.append(span)
+            while len(waiting) > LAG:
+                row_max(*waiting.pop(0))
+            for call, m in late_calls.get(i, []):
+                call(m)
 
+        near = OUT - 2 * N_CHUNK
+        end = OUT - N_CHUNK
         corner = z[:, 0:P:32]
-        for target, span in waiting[:-1]:
-            row_max(target, *span)
-        nc.vector.tensor_reduce(out=corner, in_=best[:], axis=X_AXIS, op=MAX)
-        nc.vector.tensor_scalar_mul(out=corner, in0=corner, scalar1=2.0)
-        target, span = waiting[-1]
-        row_max(target, *span)
+        before = keep.tile([P, M_TILES], F32, name="before")
+        part = keep.tile([P, 1], F32, name="part")
+        last = keep.tile([P, 1], F32, name="last")
+        row_max(*waiting.pop(0))
+        nc.vector.tensor_reduce(out=before[:, 0:3], in_=best[:, 0:3, :], axis=X_AXIS, op=MAX)
+        nc.vector.tensor_reduce(out=before[:, 3:4], in_=best[:, 3:4, 0 : CHUNKS - 4], axis=X_AXIS, op=MAX)
+        nc.scalar.mul(out=corner, in_=before[:], mul=2.0)
+        mx_group(3, near, N_CHUNK)
+        add_bias_and_gelu(nc.gpsimd, 3, 1, near // POOL, end // POOL)
+        for q in range(N_CHUNK // TAPER):
+            mx_group(3, end + q * TAPER, TAPER)
+        add_bias_and_gelu(nc.vector, 3, 1, end // POOL, OUT // POOL)
+        nc.vector.tensor_reduce(
+            out=part[:], in_=acted[:, 3, (CHUNKS - 4) * POOLED : end // POOL], axis=X_AXIS, op=MAX
+        )
+        nc.vector.tensor_scalar(
+            out=z[:, 96:97], in0=part[:], scalar1=2.0, scalar2=z[:, 96:97], op0=MULT, op1=MAX
+        )
+        nc.vector.tensor_reduce(out=last[:], in_=acted[:, 3, end // POOL : OUT // POOL], axis=X_AXIS, op=MAX)
         nc.vector.tensor_scalar(
             out=z[:, 96:97], in0=last[:], scalar1=2.0, scalar2=z[:, 96:97], op0=MULT, op1=MAX
         )

@@ -34,8 +34,9 @@ TAPER = 128
 LAG = 2
 Q = 32
 PLANE_GROUPS = ((0, 1), (1, 1), (2, 2), (4, 4))
-LATE_AFTER = {5: 2, 7: 3}
-LATE_STEPS = {2: (4, 5, 5, 6), 3: (8, 9, 9, 10)}
+EARLY = (0, 1, 2)
+LATE_AFTER = {5: 3}
+LATE_STEPS = {3: (4, 5, 5, 6)}
 
 
 def tile_modelnew_kernel(tc, x, weight_words, weight_scales, bias, out):
@@ -53,7 +54,7 @@ def tile_modelnew_kernel(tc, x, weight_words, weight_scales, bias, out):
 
         x_rows = x.rearrange("(m p) k -> m p k", p=P)
         x_sb = []
-        for m in (0, 1):
+        for m in EARLY:
             x_sb.append(keep.tile([P, IN], BF16, name="x_sb%d" % m))
             nc.sync.dma_start(out=x_sb[m][:], in_=x_rows[m])
 
@@ -128,7 +129,7 @@ def tile_modelnew_kernel(tc, x, weight_words, weight_scales, bias, out):
                     out=x_codes(m, g), scales=x_plane(m, g), in_=grouped[m][:, g].rearrange("p r t -> p (r t)")
                 )
 
-        for m in (0, 1):
+        for m in EARLY:
             words = x_sb[m][:].bitcast(F32)
             for h in range(2):
                 tp = psum.tile([P, 4, P], F32, name="tp", tag="bank")
@@ -233,11 +234,9 @@ def tile_modelnew_kernel(tc, x, weight_words, weight_scales, bias, out):
 
         units = []
         for n in range(CHUNKS):
-            units.append((((0, n), (1, n)), (0, 2, n * POOLED, (n + 1) * POOLED)))
-        for m in (2, 3):
-            for n in range(0, CHUNKS, 2):
-                units.append((((m, n), (m, n + 1)), (m, 1, n * POOLED, (n + 2) * POOLED)))
-        units = units[:-1]
+            units.append((((0, n), (1, n), (2, n)), (0, 3, n * POOLED, (n + 1) * POOLED)))
+        for n in range(0, CHUNKS - 2, 2):
+            units.append((((3, n), (3, n + 1)), (3, 1, n * POOLED, (n + 2) * POOLED)))
 
         waiting = []
         for i, (pair, span) in enumerate(units):

@@ -238,27 +238,28 @@ def tile_modelnew_kernel(tc, x, weight_words, weight_scales, bias, out):
         for n in range(0, CHUNKS - 2, 2):
             units.append((((3, n), (3, n + 1)), (3, 1, n * POOLED, (n + 2) * POOLED)))
 
+        before = keep.tile([P, M_TILES], F32, name="before")
         waiting = []
-        for i, (pair, span) in enumerate(units):
-            for m, n in pair:
+        for i, (members, span) in enumerate(units):
+            for k, (m, n) in enumerate(members):
                 mx_group(m, n * N_CHUNK, N_CHUNK)
+                if k == 0 and len(waiting) == LAG:
+                    row_max(*waiting.pop(0))
             add_bias_and_gelu(nc.gpsimd, *span)
             waiting.append(span)
-            while len(waiting) > LAG:
-                row_max(*waiting.pop(0))
             for call, m in late_calls.get(i, []):
                 call(m)
+            if i == CHUNKS + 1:
+                nc.vector.tensor_reduce(out=before[:, 0:3], in_=best[:, 0:3, :], axis=X_AXIS, op=MAX)
+                nc.scalar.mul(out=z[:, 0:96:32], in_=before[:, 0:3], mul=2.0)
 
         near = OUT - 2 * N_CHUNK
         end = OUT - N_CHUNK
-        corner = z[:, 0:P:32]
-        before = keep.tile([P, M_TILES], F32, name="before")
         part = keep.tile([P, 1], F32, name="part")
         last = keep.tile([P, 1], F32, name="last")
         row_max(*waiting.pop(0))
-        nc.vector.tensor_reduce(out=before[:, 0:3], in_=best[:, 0:3, :], axis=X_AXIS, op=MAX)
         nc.vector.tensor_reduce(out=before[:, 3:4], in_=best[:, 3:4, 0 : CHUNKS - 4], axis=X_AXIS, op=MAX)
-        nc.scalar.mul(out=corner, in_=before[:], mul=2.0)
+        nc.scalar.mul(out=z[:, 96:97], in_=before[:, 3:4], mul=2.0)
         mx_group(3, near, N_CHUNK)
         add_bias_and_gelu(nc.gpsimd, 3, 1, near // POOL, end // POOL)
         for q in range(N_CHUNK // TAPER):

@@ -33,7 +33,7 @@ PAD_WORDS = 48
 TAPER = 128
 LAG = 2
 Q = 32
-PLANE_GROUPS = ((0, 1), (1, 1), (2, 2), (4, 4))
+PLANE_GROUPS = tuple((c, 1) for c in range(CHUNKS))
 EARLY = (0, 1, 2)
 LATE_AFTER = {5: 3}
 LATE_STEPS = {3: (4, 5, 5, 6)}

@@ -70,6 +70,9 @@ def tile_modelnew_kernel(tc, x, weight_words, weight_scales, bias, out):
                 planes[first + k] = (plane_tiles[first], k)
         z = keep.tile([P, P], F32, name="z", align_bytes=64)
         nc.vector.memset(z[:], 0.0)
+        ones_two = keep.tile([P, 2 + N_CHUNK // POOL], F32, name="ones_two")
+        nc.gpsimd.memset(ones_two[:], 1.0)
+        nc.gpsimd.memset(ones_two[:, 1 + POOLED : 2 + POOLED], 2.0)
 
         bias_rows = keep.tile([P, P], BF16, name="bias_rows")
         w_i32 = weight_words.bitcast(I32)
@@ -207,7 +210,7 @@ def tile_modelnew_kernel(tc, x, weight_words, weight_scales, bias, out):
                 op=ADD,
             )
 
-        def add_bias_and_gelu(engine, m0, count, j0, j1):
+        def add_bias(engine, m0, count, j0, j1):
             engine.tensor_tensor(
                 out=biased[:, m0 : m0 + count, j0:j1].rearrange("p m (s b) -> p m s b", b=32),
                 in0=sums[:, m0 : m0 + count, j0:j1].rearrange("p m (s b) -> p m s b", b=32),
@@ -217,6 +220,9 @@ def tile_modelnew_kernel(tc, x, weight_words, weight_scales, bias, out):
                 .to_broadcast([P, count, (j1 - j0) // 32, 32]),
                 op=ADD,
             )
+
+        def add_bias_and_gelu(engine, m0, count, j0, j1):
+            add_bias(engine, m0, count, j0, j1)
             nc.scalar.activation(
                 out=acted[:, m0 : m0 + count, j0:j1],
                 in_=biased[:, m0 : m0 + count, j0:j1],
@@ -238,7 +244,7 @@ def tile_modelnew_kernel(tc, x, weight_words, weight_scales, bias, out):
         for n in range(0, CHUNKS - 2, 2):
             units.append((((3, n), (3, n + 1)), (3, 1, n * POOLED, (n + 2) * POOLED)))
 
-        before = keep.tile([P, M_TILES], F32, name="before")
+        before = keep.tile([P, 3], F32, name="before")
         waiting = []
         for i, (members, span) in enumerate(units):
             for k, (m, n) in enumerate(members):
@@ -250,34 +256,36 @@ def tile_modelnew_kernel(tc, x, weight_words, weight_scales, bias, out):
             for call, m in late_calls.get(i, []):
                 call(m)
             if i == CHUNKS + 1:
-                nc.vector.tensor_reduce(out=before[:, 0:3], in_=best[:, 0:3, :], axis=X_AXIS, op=MAX)
-                nc.scalar.mul(out=z[:, 0:96:32], in_=before[:, 0:3], mul=2.0)
+                nc.vector.tensor_reduce(out=before[:], in_=best[:, 0:3, :], axis=X_AXIS, op=MAX)
+                nc.scalar.mul(out=z[:, 0:96:32], in_=before[:], mul=2.0)
 
         near = OUT - 2 * N_CHUNK
         end = OUT - N_CHUNK
-        part = keep.tile([P, 1], F32, name="part")
-        last = keep.tile([P, 1], F32, name="last")
+        out_rows = out.rearrange("(m a r) -> a m r", a=4, r=32)
+        z_t = keep.tile([P, P], F32, name="z_t", align_bytes=64)
+        finals = keep.tile([P, 2 + POOLED], F32, name="finals")
+        scanned = keep.tile([P, 160], F32, name="scanned", align_bytes=64)
+        scanned_t = keep.tile([P, 32], F32, name="scanned_t", align_bytes=64)
         row_max(*waiting.pop(0))
-        nc.vector.tensor_reduce(out=before[:, 3:4], in_=best[:, 3:4, 0 : CHUNKS - 4], axis=X_AXIS, op=MAX)
-        nc.scalar.mul(out=z[:, 96:97], in_=before[:, 3:4], mul=2.0)
+        nc.vector.transpose(out=z_t[:], in_=z[:])
+        nc.sync.dma_start(out=out_rows[:, 0:3], in_=z_t[0:P:32, 0:96].rearrange("a (m r) -> a m r", r=32))
+        nc.vector.tensor_reduce(out=finals[:, 0:1], in_=best[:, 3:4, 0 : CHUNKS - 4], axis=X_AXIS, op=MAX)
         mx_group(3, near, N_CHUNK)
         add_bias_and_gelu(nc.gpsimd, 3, 1, near // POOL, end // POOL)
         for q in range(N_CHUNK // TAPER):
             mx_group(3, end + q * TAPER, TAPER)
-        add_bias_and_gelu(nc.vector, 3, 1, end // POOL, OUT // POOL)
+        add_bias(nc.vector, 3, 1, end // POOL, OUT // POOL)
+        nc.scalar.activation(
+            out=finals[:, 2 : 2 + POOLED],
+            in_=biased[:, 3, end // POOL : OUT // POOL],
+            func=GELU,
+            scale=1.0 / POOL,
+        )
         nc.vector.tensor_reduce(
-            out=part[:], in_=acted[:, 3, (CHUNKS - 4) * POOLED : end // POOL], axis=X_AXIS, op=MAX
+            out=finals[:, 1:2], in_=acted[:, 3, (CHUNKS - 4) * POOLED : end // POOL], axis=X_AXIS, op=MAX
         )
-        nc.vector.tensor_scalar(
-            out=z[:, 96:97], in0=part[:], scalar1=2.0, scalar2=z[:, 96:97], op0=MULT, op1=MAX
+        nc.vector.tensor_tensor_scan(
+            out=scanned[:, 30:160], data0=finals[:], data1=ones_two[:], initial=finals[:, 0:1], op0=MAX, op1=MULT
         )
-        nc.vector.tensor_reduce(out=last[:], in_=acted[:, 3, end // POOL : OUT // POOL], axis=X_AXIS, op=MAX)
-        nc.vector.tensor_scalar(
-            out=z[:, 96:97], in0=last[:], scalar1=2.0, scalar2=z[:, 96:97], op0=MULT, op1=MAX
-        )
-        z_t = keep.tile([P, P], F32, name="z_t", align_bytes=64)
-        nc.vector.transpose(out=z_t[:], in_=z[:])
-        nc.sync.dma_start(
-            out=out.rearrange("(m a r) -> a m r", a=4, r=32),
-            in_=z_t[0:P:32, :].rearrange("a (m r) -> a m r", r=32),
-        )
+        nc.vector.transpose(out=scanned_t[:], in_=scanned[:, 128:160])
+        nc.sync.dma_start(out=out_rows[:, 3], in_=scanned_t[31:P:32, :])

@@ -34,6 +34,8 @@ TAPER = 128
 LAG = 2
 Q = 32
 PLANE_GROUPS = tuple((c, 1) for c in range(CHUNKS))
+BUSY_FIRST = 4
+BUSY_BEHIND = 2
 EARLY = (0, 1, 2)
 LATE_AFTER = {5: 3}
 LATE_STEPS = {3: (4, 5, 5, 6)}
@@ -46,6 +48,8 @@ def tile_modelnew_kernel(tc, x, weight_words, weight_scales, bias, out):
         psum = ctx.enter_context(tc.psum_pool(name="psum", bufs=8))
         ctx.enter_context(tc.manual_schedule())
 
+        zeros = keep.tile([P, N_CHUNK], BF16, name="zeros")
+        nc.vector.memset(zeros[:], 0.0)
         warm = keep.tile([P, 1], F32, name="warm")
         nc.vector.memset(warm[:], 0.0)
         nc.scalar.activation(out=warm[:], in_=warm[:], func=GELU)
@@ -132,6 +136,13 @@ def tile_modelnew_kernel(tc, x, weight_words, weight_scales, bias, out):
                     out=x_codes(m, g), scales=x_plane(m, g), in_=grouped[m][:, g].rearrange("p r t -> p (r t)")
                 )
 
+        idle_bank = psum.tile([P, N_CHUNK], F32, name="idle_bank", tag="bank")
+
+        def keep_busy(count):
+            for q in range(count):
+                nc.tensor.matmul(out=idle_bank[:], lhsT=zeros[:, 0:P], rhs=zeros[:], start=True, stop=True)
+
+        keep_busy(BUSY_FIRST)
         for m in EARLY:
             words = x_sb[m][:].bitcast(F32)
             for h in range(2):
@@ -149,6 +160,8 @@ def tile_modelnew_kernel(tc, x, weight_words, weight_scales, bias, out):
                     out=grouped[m][:].bitcast(F32)[:, 2 * h : 2 * h + 2],
                     in_=tp[:].rearrange("p (g u) r -> p g r u", u=2),
                 )
+            if m < EARLY[-1]:
+                keep_busy(BUSY_BEHIND)
             quantise(m)
 
         split = {}

from contextlib import ExitStack

import concourse.mybir as mybir
from concourse.masks import make_identity

FLOPS = 2 * 512 * 2048 * 4096

F32 = mybir.dt.float32
BF16 = mybir.dt.bfloat16
I32 = mybir.dt.int32
U8 = mybir.dt.uint8
U32 = mybir.dt.uint32
FP8X4 = mybir.dt.float8_e4m3fn_x4
FP4X4 = mybir.dt.float4_e2m1fn_x4
ADD = mybir.AluOpType.add
MAX = mybir.AluOpType.max
MULT = mybir.AluOpType.mult
X_AXIS = mybir.AxisListType.X
GELU = mybir.ActivationFunctionType.Gelu_apprx_tanh

P = 128
ROWS = 512
IN = 2048
OUT = 4096
POOL = 4
M_TILES = ROWS // P
K_PASS = 4 * P
G = IN // K_PASS
N_CHUNK = 512
CHUNKS = OUT // N_CHUNK
POOLED = N_CHUNK // POOL
PAD_WORDS = 48
TAPER = 128
LAG = 2
Q = 32
PLANE_GROUPS = tuple((c, 1) for c in range(CHUNKS))
BUSY_FIRST = 4
BUSY_BEHIND = 2
EARLY = (0, 1, 2)
LATE_AFTER = {5: 3}
LATE_STEPS = {3: (4, 5, 5, 6)}


def tile_modelnew_kernel(tc, x, weight_words, weight_scales, bias, out):
    nc = tc.nc
    with ExitStack() as ctx:
        keep = ctx.enter_context(tc.tile_pool(name="keep", bufs=1))
        psum = ctx.enter_context(tc.psum_pool(name="psum", bufs=8))
        ctx.enter_context(tc.manual_schedule())

        zeros = keep.tile([P, N_CHUNK], BF16, name="zeros")
        nc.vector.memset(zeros[:], 0.0)
        warm = keep.tile([P, 1], F32, name="warm")
        nc.vector.memset(warm[:], 0.0)
        nc.scalar.activation(out=warm[:], in_=warm[:], func=GELU)
        ident = keep.tile([P, P], F32, name="ident")
        make_identity(nc, ident[:])

        x_rows = x.rearrange("(m p) k -> m p k", p=P)
        x_sb = []
        for m in EARLY:
            x_sb.append(keep.tile([P, IN], BF16, name="x_sb%d" % m))
            nc.sync.dma_start(out=x_sb[m][:], in_=x_rows[m])

        w_tiles = []
        for c in range(CHUNKS):
            w_tiles.append(keep.tile([P, G, 2 * N_CHUNK], U8, name="w%d" % c, align_bytes=256))
        planes = {}
        plane_tiles = {}
        for first, count in PLANE_GROUPS:
            plane_tiles[first] = keep.tile([P, G, count * N_CHUNK], U8, name="plane%d" % first, align_bytes=256)
            nc.vector.memset(plane_tiles[first][:].bitcast(I32), 0)
            for k in range(count):
                planes[first + k] = (plane_tiles[first], k)
        z = keep.tile([P, P], F32, name="z", align_bytes=64)
        nc.vector.memset(z[:], 0.0)
        ones_two = keep.tile([P, 2 + N_CHUNK // POOL], F32, name="ones_two")
        nc.gpsimd.memset(ones_two[:], 1.0)
        nc.gpsimd.memset(ones_two[:, 1 + POOLED : 2 + POOLED], 2.0)

        bias_rows = keep.tile([P, P], BF16, name="bias_rows")
        w_i32 = weight_words.bitcast(I32)
        s_i32 = weight_scales.bitcast(I32)
        x_blocks = x.rearrange("r k -> (r k)").rearrange(
            "(m j y a e) -> m a j y e", m=M_TILES, j=Q, y=4 * G, a=P // Q
        )
        x_late = {}
        for c in range(CHUNKS):
            if c in plane_tiles:
                s_lo = c * N_CHUNK // 4
                s_hi = s_lo + plane_tiles[c].shape[2] // 4
                for r in range(4):
                    nc.sync.dma_start(
                        out=plane_tiles[c][:].bitcast(I32)[r:P:32],
                        in_=s_i32[:, r:16:4, s_lo:s_hi].rearrange("g q c -> q g c"),
                    )
            w_lo = c * 2 * N_CHUNK // 4
            w_hi = (c + 1) * 2 * N_CHUNK // 4
            if c == 0:
                for g in range(0, G, 2):
                    nc.sync.dma_start(
                        out=w_tiles[c][:, g : g + 2, :].bitcast(I32),
                        in_=w_i32[g : g + 2, :, w_lo:w_hi].rearrange("g p b -> p g b"),
                    )
                nc.sync.dma_start(
                    out=bias_rows[:],
                    in_=bias.rearrange("(s i) -> s i", i=P).unsqueeze(0).to_broadcast([4, 32, P]),
                )
            else:
                nc.sync.dma_start(
                    out=w_tiles[c][:].bitcast(I32),
                    in_=w_i32[:, :, w_lo:w_hi].rearrange("g p b -> p g b"),
                )
            if c in LATE_AFTER:
                m = LATE_AFTER[c]
                x_late[m] = keep.tile([P, 4 * G, P], BF16, name="x_late%d" % m, align_bytes=64)
                for a in range(P // Q):
                    nc.sync.dma_start(out=x_late[m][Q * a : Q * (a + 1)], in_=x_blocks[m, a])

        codes = keep.tile([P, PAD_WORDS + M_TILES * G * P], U32, name="codes", align_bytes=256)
        x_scales = keep.tile([P, M_TILES * G, 2 * P], U8, name="x_scales", align_bytes=256)
        grouped = []
        for m in range(M_TILES):
            grouped.append(keep.tile([P, G, P, 4], BF16, name="grouped%d" % m, align_bytes=64))

        def x_codes(m, g):
            lo = PAD_WORDS + (m * G + g) * P
            return codes[:, lo : lo + P].bitcast(FP8X4)

        def x_plane(m, g):
            return x_scales[:, m * G + g, 0:P]

        def quantise(m):
            for g in range(G):
                nc.vector.quantize_mx(
                    out=x_codes(m, g), scales=x_plane(m, g), in_=grouped[m][:, g].rearrange("p r t -> p (r t)")
                )

        idle_bank = psum.tile([P, N_CHUNK], F32, name="idle_bank", tag="bank")

        def keep_busy(count):
            for q in range(count):
                nc.tensor.matmul(out=idle_bank[:], lhsT=zeros[:, 0:P], rhs=zeros[:], start=True, stop=True)

        keep_busy(BUSY_FIRST)
        for m in EARLY:
            words = x_sb[m][:].bitcast(F32)
            for h in range(2):
                tp = psum.tile([P, 4, P], F32, name="tp", tag="bank")
                for g2 in range(2):
                    g = 2 * h + g2
                    for u in range(2):
                        nc.tensor.transpose(
                            out=tp[:, 2 * g2 + u, :],
                            in_=words[:, 256 * g + u : 256 * (g + 1) : 2],
                            identity=ident[:],
                        )
                copy_out = nc.vector.tensor_copy if h == 0 else nc.scalar.copy
                copy_out(
                    out=grouped[m][:].bitcast(F32)[:, 2 * h : 2 * h + 2],
                    in_=tp[:].rearrange("p (g u) r -> p g r u", u=2),
                )
            if m < EARLY[-1]:
                keep_busy(BUSY_BEHIND)
            quantise(m)

        split = {}
        turned = {}

        def late_split(m):
            split[m] = keep.tile([P, 4 * G, 2, Q], F32, name="split%d" % m, align_bytes=64)
            words = x_late[m][:].rearrange("p y e -> p (y e)").bitcast(F32)
            nc.scalar.copy(out=split[m][:], in_=words.rearrange("p (y i u) -> p y u i", i=Q, u=2))

        def late_turn(m):
            turned[m] = keep.tile([P, 4 * G * 2 * Q], F32, name="turned%d" % m, align_bytes=64)
            nc.vector.transpose(out=turned[m][:], in_=split[m][:].rearrange("p y u i -> p (y u i)"))

        def late_group(m):
            source = turned[m][:].rearrange("p (b g u j) -> p g j b u", b=4, g=G, u=2)
            target = grouped[m][:].bitcast(F32)
            for g in range(G):
                nc.scalar.copy(out=target[:, g].rearrange("p (j b) u -> p j b u", b=4), in_=source[:, g])

        late_calls = {}
        for m in LATE_STEPS:
            for step, call in zip(LATE_STEPS[m], (late_split, late_turn, late_group, quantise)):
                late_calls.setdefault(step, []).append((call, m))

        bias_sum = keep.tile([P, 32], F32, name="bias_sum")
        nc.vector.tensor_reduce(
            out=bias_sum[:], in_=bias_rows[:].rearrange("p (b c) -> p b c", c=POOL), axis=X_AXIS, op=ADD
        )
        bias_rep = keep.tile([P, 32, 32], F32, name="bias_rep", align_bytes=64)
        nc.vector.tensor_copy(out=bias_rep[:], in_=bias_sum[:].unsqueeze(2).to_broadcast([P, 32, 32]))
        bias_t = keep.tile([P, 1024], F32, name="bias_t", align_bytes=64)
        nc.vector.transpose(out=bias_t[:], in_=bias_rep[:].rearrange("p b r -> p (b r)"))

        sums = keep.tile([P, M_TILES, OUT // POOL], F32, name="sums")
        biased = keep.tile([P, M_TILES, OUT // POOL], F32, name="biased")
        acted = keep.tile([P, M_TILES, OUT // POOL], F32, name="acted")
        best = keep.tile([P, M_TILES, CHUNKS], F32, name="best")

        def mx_group(m, col, width):
            c = col // N_CHUNK
            lo = col % N_CHUNK
            plane, k = planes[c]
            acc = psum.tile([P, width], F32, name="acc", tag="bank")
            for g in range(G):
                nc.tensor.matmul_mx(
                    out=acc[:],
                    lhsT=x_codes(m, g),
                    lhsT_scale=x_plane(m, g),
                    rhs=w_tiles[c][:, g, 2 * lo : 2 * (lo + width)].bitcast(FP4X4),
                    rhs_scale=plane[:, g, k * N_CHUNK + lo : k * N_CHUNK + lo + width],
                    start=(g == 0),
                    stop=(g == G - 1),
                )
            nc.vector.tensor_reduce(
                out=sums[:, m, col // POOL : (col + width) // POOL],
                in_=acc[:].rearrange("p (j c) -> p j c", c=POOL),
                axis=X_AXIS,
                op=ADD,
            )

        def add_bias(engine, m0, count, j0, j1):
            engine.tensor_tensor(
                out=biased[:, m0 : m0 + count, j0:j1].rearrange("p m (s b) -> p m s b", b=32),
                in0=sums[:, m0 : m0 + count, j0:j1].rearrange("p m (s b) -> p m s b", b=32),
                in1=bias_t[:]
                .rearrange("p (b s) -> p s b", s=32)[:, j0 // 32 : j1 // 32, :]
                .unsqueeze(1)
                .to_broadcast([P, count, (j1 - j0) // 32, 32]),
                op=ADD,
            )

        def add_bias_and_gelu(engine, m0, count, j0, j1):
            add_bias(engine, m0, count, j0, j1)
            nc.scalar.activation(
                out=acted[:, m0 : m0 + count, j0:j1],
                in_=biased[:, m0 : m0 + count, j0:j1],
                func=GELU,
                scale=1.0 / POOL,
            )

        def row_max(m0, count, j0, j1):
            nc.vector.tensor_reduce(
                out=best[:, m0 : m0 + count, j0 // POOLED : j1 // POOLED],
                in_=acted[:, m0 : m0 + count, j0:j1].rearrange("p m (n j) -> p m n j", j=POOLED),
                axis=X_AXIS,
                op=MAX,
            )

        units = []
        for n in range(CHUNKS):
            units.append((((0, n), (1, n), (2, n)), (0, 3, n * POOLED, (n + 1) * POOLED)))
        for n in range(0, CHUNKS - 2, 2):
            units.append((((3, n), (3, n + 1)), (3, 1, n * POOLED, (n + 2) * POOLED)))

        before = keep.tile([P, 3], F32, name="before")
        waiting = []
        for i, (members, span) in enumerate(units):
            for k, (m, n) in enumerate(members):
                mx_group(m, n * N_CHUNK, N_CHUNK)
                if k == 0 and len(waiting) == LAG:
                    row_max(*waiting.pop(0))
            add_bias_and_gelu(nc.gpsimd, *span)
            waiting.append(span)
            for call, m in late_calls.get(i, []):
                call(m)
            if i == CHUNKS + 1:
                nc.vector.tensor_reduce(out=before[:], in_=best[:, 0:3, :], axis=X_AXIS, op=MAX)
                nc.scalar.mul(out=z[:, 0:96:32], in_=before[:], mul=2.0)

        near = OUT - 2 * N_CHUNK
        end = OUT - N_CHUNK
        out_rows = out.rearrange("(m a r) -> a m r", a=4, r=32)
        z_t = keep.tile([P, P], F32, name="z_t", align_bytes=64)
        finals = keep.tile([P, 2 + POOLED], F32, name="finals")
        scanned = keep.tile([P, 160], F32, name="scanned", align_bytes=64)
        scanned_t = keep.tile([P, 32], F32, name="scanned_t", align_bytes=64)
        row_max(*waiting.pop(0))
        nc.vector.transpose(out=z_t[:], in_=z[:])
        nc.sync.dma_start(out=out_rows[:, 0:3], in_=z_t[0:P:32, 0:96].rearrange("a (m r) -> a m r", r=32))
        nc.vector.tensor_reduce(out=finals[:, 0:1], in_=best[:, 3:4, 0 : CHUNKS - 4], axis=X_AXIS, op=MAX)
        mx_group(3, near, N_CHUNK)
        add_bias_and_gelu(nc.gpsimd, 3, 1, near // POOL, end // POOL)
        for q in range(N_CHUNK // TAPER):
            mx_group(3, end + q * TAPER, TAPER)
        add_bias(nc.vector, 3, 1, end // POOL, OUT // POOL)
        nc.scalar.activation(
            out=finals[:, 2 : 2 + POOLED],
            in_=biased[:, 3, end // POOL : OUT // POOL],
            func=GELU,
            scale=1.0 / POOL,
        )
        nc.vector.tensor_reduce(
            out=finals[:, 1:2], in_=acted[:, 3, (CHUNKS - 4) * POOLED : end // POOL], axis=X_AXIS, op=MAX
        )
        nc.vector.tensor_tensor_scan(
            out=scanned[:, 30:160], data0=finals[:], data1=ones_two[:], initial=finals[:, 0:1], op0=MAX, op1=MULT
        )
        nc.vector.transpose(out=scanned_t[:], in_=scanned[:, 128:160])
        nc.sync.dma_start(out=out_rows[:, 3], in_=scanned_t[31:P:32, :])
